import numpy as np
import ml_dtypes


def mxq(x, axis, fmt="e4m3"):
    dtype, down = {"e4m3": (ml_dtypes.float8_e4m3fn, 7), "e5m2": (ml_dtypes.float8_e5m2, 14)}[fmt]
    v = np.moveaxis(np.asarray(x, np.float32).astype(ml_dtypes.bfloat16).astype(np.float64), axis, -1)
    blocks = v.reshape(v.shape[:-1] + (-1, 32))
    amax = np.abs(blocks).max(-1, keepdims=True)
    byte = np.maximum(np.where(amax > 0, np.frexp(amax)[1] - 1 + 127, 0) - down, 1)
    scale = np.exp2(byte - 127.0)
    codes = (blocks / scale).astype(np.float32).astype(dtype).astype(np.float64)
    return np.moveaxis((codes * scale).reshape(v.shape), -1, axis)


WIDE = False


def mx_kscale(k):
    if not WIDE:
        return np.ones(k)
    levels = np.array([20, -20, 10, -10, 0])
    a = np.random.permutation(np.resize(levels, k // 512 * 4)).reshape(k // 512, 4)
    idx = np.arange(k)
    return np.exp2(a[idx // 512, idx % 128 // 32])


BF16 = ml_dtypes.bfloat16


def bf(x):
    return np.asarray(x, np.float32).astype(BF16)


def f64(x):
    return np.asarray(x).astype(np.float64)


B, S, HID, NH, NOPE, ROPE, VD, KV_RANK, SW, QB = 1, 8192, 256, 8, 64, 128, 128, 512, 384, 128
QK = NOPE + ROPE


def rotate_half(x):
    h = x.shape[-1] // 2
    return np.concatenate([-x[..., h:], x[..., :h]], axis=-1)


def rotate_half_t(x):
    h = x.shape[-1] // 2
    return np.concatenate([x[..., h:], -x[..., :h]], axis=-1)


def rope_tables():
    pos = np.arange(S, dtype=np.float64)
    inv = 1.0 / (10000.0 ** (np.arange(0, ROPE, 2, dtype=np.float64) / ROPE))
    ang = pos[:, None] * inv[None, :]
    ang = np.concatenate([ang, ang], axis=-1)
    return bf(np.broadcast_to(np.cos(ang)[None], (B, S, ROPE))), bf(np.broadcast_to(np.sin(ang)[None], (B, S, ROPE)))


def setup_inputs():
    s = mx_kscale(S)
    cos, sin = rope_tables()
    hs = np.random.standard_normal((B, S, HID)) * s[None, :, None]
    wq = np.random.standard_normal((HID, NH * QK)) * 2.0 / np.sqrt(HID)
    bq = np.random.standard_normal(NH * QK) * 0.2
    g = np.random.standard_normal((B, NH, S, QK)) * np.exp2(np.random.randint(-12, 1, (B, 1, S, 1))) / s[None, None, :, None]
    return {"hidden_states": bf(hs), "cos": cos, "sin": sin, "Wq": bf(wq), "bq": bf(bq), "grad_out": bf(g)}


def reference(hidden_states, cos, sin, Wq, bq, grad_out):
    g = f64(grad_out)
    c, si = f64(cos)[:, None], f64(sin)[:, None]
    g_nope, g_rope = g[..., :NOPE], g[..., NOPE:]
    d_rope = g_rope * c + rotate_half_t(g_rope * si)
    dq = np.concatenate([g_nope, d_rope], axis=-1).transpose(0, 2, 1, 3).reshape(B * S, NH * QK)
    x = f64(hidden_states).reshape(B * S, HID)
    return mxq(x, 0, "e4m3").T @ mxq(dq, 0, "e5m2")

@@ -1,0 +1,200 @@
+from contextlib import ExitStack
+
+import concourse.mybir as mybir
+from concourse.masks import make_identity
+
+BF16 = mybir.dt.bfloat16
+F32 = mybir.dt.float32
+U32 = mybir.dt.uint32
+U8 = mybir.dt.uint8
+E4M3_X4 = mybir.dt.float8_e4m3fn_x4
+E5M2_X4 = mybir.dt.float8_e5m2_x4
+ALU = mybir.AluOpType
+
+P = 128
+PACK = 4
+K_PASS = P * PACK
+
+TOKENS = 8192
+HIDDEN = 256
+HEADS = 8
+PLAIN = 64
+ROTATED = 128
+HALF = ROTATED // 2
+HEAD_COLS = PLAIN + ROTATED
+DQ_COLS = HEADS * HEAD_COLS
+
+PASSES = TOKENS // K_PASS
+UNIT_HEADS = 4
+UNITS_PER_PASS = HEADS // UNIT_HEADS
+UNITS = PASSES * UNITS_PER_PASS
+UNIT_COLS = UNIT_HEADS * HEAD_COLS
+M_TILE = 128
+N_TILE = 512
+M_TILES = HIDDEN // M_TILE
+N_TILES = DQ_COLS // N_TILE
+LOADS_AHEAD = 3
+
+FLOPS = 2 * TOKENS * HIDDEN * DQ_COLS
+BYTES = 2 * TOKENS * (HIDDEN + 2 * ROTATED + DQ_COLS) + 4 * HIDDEN * DQ_COLS
+
+
+def column_cuts(first, last):
+    inner = [c for c in range(first + 1, last) if c % N_TILE == 0]
+    return [first] + inner + [last]
+
+
+def tile_gptossmlaattention_pb_k_kernel(tc, hidden_states, cos, sin, Wq, bq, grad_out, out):
+    nc = tc.nc
+    with ExitStack() as stack:
+        const = stack.enter_context(tc.tile_pool(name="const", bufs=1))
+        loads = stack.enter_context(tc.tile_pool(name="loads", bufs=3))
+        work = stack.enter_context(tc.tile_pool(name="work", bufs=3))
+        tables_psum = stack.enter_context(tc.psum_pool(name="tables_psum", bufs=1))
+        acc_psum = stack.enter_context(tc.psum_pool(name="acc_psum", bufs=1))
+        stack.enter_context(tc.manual_schedule())
+
+        identity = const.tile([P, P], BF16, name="identity")
+        make_identity(nc, identity[:])
+
+        acc = {}
+        for m in range(M_TILES):
+            for n in range(N_TILES):
+                acc[m, n] = acc_psum.tile([M_TILE, N_TILE], F32, name="acc_%d_%d" % (m, n))
+
+        cos_sb, sin_sb, x_raw = {}, {}, {}
+        cos_ps, sin_ps = {}, {}
+        g = {}
+        r_cos, r_sin = {}, {}
+        x_grouped, dq_grouped = {}, {}
+        x_codes, x_scales, dq_codes, dq_scales = {}, {}, {}, {}
+
+        def load(u):
+            i, a = divmod(u, UNITS_PER_PASS)
+            tokens = slice(i * K_PASS, (i + 1) * K_PASS)
+            if a == 0:
+                cos_sb[i] = loads.tile([P, PACK, ROTATED], BF16, name="cos_sb")
+                sin_sb[i] = loads.tile([P, PACK, ROTATED], BF16, name="sin_sb")
+                nc.sync.dma_start(out=cos_sb[i][:], in_=cos[0, tokens, :].rearrange("(p t) j -> p t j", t=PACK))
+                nc.sync.dma_start(out=sin_sb[i][:], in_=sin[0, tokens, :].rearrange("(p t) j -> p t j", t=PACK))
+            heads = slice(a * UNIT_HEADS, (a + 1) * UNIT_HEADS)
+            g[u] = loads.tile([P, UNIT_HEADS, PACK, HEAD_COLS], BF16, name="g", bufs=LOADS_AHEAD + 3)
+            nc.sync.dma_start(out=g[u][:], in_=grad_out[0, heads, tokens, :].rearrange("h (p t) c -> p h t c", t=PACK))
+            if a == 0:
+                x_raw[i] = loads.tile([P, PACK, HIDDEN], BF16, name="x_raw")
+                nc.sync.dma_start(
+                    out=x_raw[i][:], in_=hidden_states[0, tokens, :].rearrange("(p t) c -> p t c", t=PACK)
+                )
+
+        def stage_tables(i):
+            cos_ps[i] = tables_psum.tile([P, PACK, ROTATED], F32, name="cos_ps")
+            sin_ps[i] = tables_psum.tile([P, PACK, ROTATED], F32, name="sin_ps")
+            for table_ps, table_sb in ((cos_ps[i], cos_sb[i]), (sin_ps[i], sin_sb[i])):
+                nc.tensor.matmul(
+                    out=table_ps[:].rearrange("p t j -> p (t j)"),
+                    lhsT=identity[:],
+                    rhs=table_sb[:].rearrange("p t j -> p (t j)"),
+                    start=True,
+                    stop=True,
+                )
+
+        def multiply(u):
+            i = u // UNITS_PER_PASS
+            shape = [P, UNIT_HEADS, PACK, ROTATED]
+            r = g[u][:, :, :, PLAIN:HEAD_COLS]
+            r_cos[u] = work.tile(shape, F32, name="r_cos")
+            r_sin[u] = work.tile(shape, F32, name="r_sin")
+            nc.vector.tensor_tensor(out=r_cos[u][:], in0=r, in1=cos_ps[i][:].unsqueeze(1).to_broadcast(shape), op=ALU.mult)
+            nc.vector.tensor_tensor(out=r_sin[u][:], in0=r, in1=sin_ps[i][:].unsqueeze(1).to_broadcast(shape), op=ALU.mult)
+
+        def combine(u):
+            low, high = slice(0, HALF), slice(HALF, ROTATED)
+            nc.gpsimd.tensor_tensor(
+                out=g[u][:, :, :, PLAIN : PLAIN + HALF],
+                in0=r_cos[u][:, :, :, low],
+                in1=r_sin[u][:, :, :, high],
+                op=ALU.add,
+            )
+            nc.gpsimd.tensor_tensor(
+                out=g[u][:, :, :, PLAIN + HALF : HEAD_COLS],
+                in0=r_cos[u][:, :, :, high],
+                in1=r_sin[u][:, :, :, low],
+                op=ALU.subtract,
+            )
+
+        def regroup(u):
+            i, a = divmod(u, UNITS_PER_PASS)
+            if a == 0:
+                x_grouped[i] = work.tile([P, HIDDEN, PACK], BF16, name="x_grouped", align_bytes=64)
+                nc.scalar.copy(out=x_grouped[i][:], in_=x_raw[i][:].rearrange("p t c -> p c t"))
+            dq_grouped[u] = work.tile([P, UNIT_COLS, PACK], BF16, name="dq_grouped", align_bytes=64)
+            nc.scalar.copy(
+                out=dq_grouped[u][:].rearrange("p (h c) t -> p h c t", h=UNIT_HEADS),
+                in_=g[u][:].rearrange("p h t c -> p h c t"),
+            )
+
+        def quantise(u):
+            i, a = divmod(u, UNITS_PER_PASS)
+            if a == 0:
+                x_codes[i] = work.tile([P, HIDDEN], U32, name="x_codes", align_bytes=64)
+                x_scales[i] = work.tile([P, HIDDEN], U8, name="x_scales", align_bytes=64)
+                dq_codes[i] = work.tile([P, DQ_COLS], U32, name="dq_codes", align_bytes=64)
+                dq_scales[i] = work.tile([P, DQ_COLS], U8, name="dq_scales", align_bytes=64)
+                nc.vector.quantize_mx(
+                    out=x_codes[i][:].bitcast(E4M3_X4),
+                    scales=x_scales[i][:],
+                    in_=x_grouped[i][:].rearrange("p c t -> p (c t)"),
+                )
+            first = a * UNIT_COLS
+            cuts = column_cuts(first, first + UNIT_COLS)
+            for lo, hi in zip(cuts[:-1], cuts[1:]):
+                nc.vector.quantize_mx(
+                    out=dq_codes[i][:, lo:hi].bitcast(E5M2_X4),
+                    scales=dq_scales[i][:, lo:hi],
+                    in_=dq_grouped[u][:, lo - first : hi - first, :].rearrange("p c t -> p (c t)"),
+                )
+
+        def contract(u):
+            i, a = divmod(u, UNITS_PER_PASS)
+            first = a * UNIT_COLS
+            for n in range(N_TILES):
+                if not first < (n + 1) * N_TILE <= first + UNIT_COLS:
+                    continue
+                n_cols = slice(n * N_TILE, (n + 1) * N_TILE)
+                for m in range(M_TILES):
+                    m_cols = slice(m * M_TILE, (m + 1) * M_TILE)
+                    nc.tensor.matmul_mx(
+                        out=acc[m, n][:],
+                        lhsT=x_codes[i][:, m_cols].bitcast(E4M3_X4),
+                        lhsT_scale=x_scales[i][:, m_cols],
+                        rhs=dq_codes[i][:, n_cols].bitcast(E5M2_X4),
+                        rhs_scale=dq_scales[i][:, n_cols],
+                        start=(i == 0),
+                        stop=(i == PASSES - 1),
+                    )
+
+        for u in range(LOADS_AHEAD):
+            load(u)
+        stage_tables(0)
+        for step in range(UNITS + 3):
+            if step + LOADS_AHEAD < UNITS:
+                load(step + LOADS_AHEAD)
+            if step < UNITS:
+                multiply(step)
+                if (step + 1) % UNITS_PER_PASS == 0 and step + 1 < UNITS:
+                    stage_tables((step + 1) // UNITS_PER_PASS)
+            if 0 <= step - 1 < UNITS:
+                combine(step - 1)
+            if 0 <= step - 2 < UNITS:
+                regroup(step - 2)
+            if 0 <= step - 3:
+                quantise(step - 3)
+                contract(step - 3)
+
+        for index, (m, n) in enumerate(sorted(acc)):
+            result = work.tile([M_TILE, N_TILE], F32, name="result", bufs=M_TILES * N_TILES)
+            if index % 2 == 0:
+                nc.vector.tensor_copy(out=result[:], in_=acc[m, n][:])
+            else:
+                nc.scalar.copy(out=result[:], in_=acc[m, n][:])
+            nc.sync.dma_start(out=out[m * M_TILE : (m + 1) * M_TILE, n * N_TILE : (n + 1) * N_TILE], in_=result[:])

@@ -56,6 +56,8 @@ def tile_gptossmlaattention_pb_k_kernel(tc, hidden_states, cos, sin, Wq, bq, gra
 
         identity = const.tile([P, P], BF16, name="identity")
         make_identity(nc, identity[:])
+        minus_identity = const.tile([P, P], BF16, name="minus_identity")
+        nc.vector.tensor_scalar_mul(out=minus_identity[:], in0=identity[:], scalar1=-1.0)
 
         acc = {}
         for m in range(M_TILES):
@@ -63,9 +65,9 @@ def tile_gptossmlaattention_pb_k_kernel(tc, hidden_states, cos, sin, Wq, bq, gra
                 acc[m, n] = acc_psum.tile([M_TILE, N_TILE], F32, name="acc_%d_%d" % (m, n))
 
         cos_sb, sin_sb, x_raw = {}, {}, {}
-        cos_ps, sin_ps = {}, {}
+        cos_ps, crossed_sin_ps = {}, {}
         g = {}
-        r_cos, r_sin = {}, {}
+        straight, crossed = {}, {}
         x_grouped, dq_grouped = {}, {}
         x_codes, x_scales, dq_codes, dq_scales = {}, {}, {}, {}
 
@@ -86,40 +88,41 @@ def tile_gptossmlaattention_pb_k_kernel(tc, hidden_states, cos, sin, Wq, bq, gra
                     out=x_raw[i][:], in_=hidden_states[0, tokens, :].rearrange("(p t) c -> p t c", t=PACK)
                 )
 
+        low, high = slice(0, HALF), slice(HALF, ROTATED)
+
         def stage_tables(i):
             cos_ps[i] = tables_psum.tile([P, PACK, ROTATED], F32, name="cos_ps")
-            sin_ps[i] = tables_psum.tile([P, PACK, ROTATED], F32, name="sin_ps")
-            for table_ps, table_sb in ((cos_ps[i], cos_sb[i]), (sin_ps[i], sin_sb[i])):
-                nc.tensor.matmul(
-                    out=table_ps[:].rearrange("p t j -> p (t j)"),
-                    lhsT=identity[:],
-                    rhs=table_sb[:].rearrange("p t j -> p (t j)"),
-                    start=True,
-                    stop=True,
-                )
+            crossed_sin_ps[i] = tables_psum.tile([P, PACK, ROTATED], F32, name="crossed_sin_ps")
+            nc.tensor.matmul(out=cos_ps[i][:], lhsT=identity[:], rhs=cos_sb[i][:], start=True, stop=True)
+            nc.tensor.matmul(
+                out=crossed_sin_ps[i][:, :, low], lhsT=identity[:], rhs=sin_sb[i][:, :, high], start=True, stop=True
+            )
+            nc.tensor.matmul(
+                out=crossed_sin_ps[i][:, :, high], lhsT=minus_identity[:], rhs=sin_sb[i][:, :, low], start=True, stop=True
+            )
 
         def multiply(u):
             i = u // UNITS_PER_PASS
-            shape = [P, UNIT_HEADS, PACK, ROTATED]
             r = g[u][:, :, :, PLAIN:HEAD_COLS]
-            r_cos[u] = work.tile(shape, F32, name="r_cos")
-            r_sin[u] = work.tile(shape, F32, name="r_sin")
-            nc.vector.tensor_tensor(out=r_cos[u][:], in0=r, in1=cos_ps[i][:].unsqueeze(1).to_broadcast(shape), op=ALU.mult)
-            nc.vector.tensor_tensor(out=r_sin[u][:], in0=r, in1=sin_ps[i][:].unsqueeze(1).to_broadcast(shape), op=ALU.mult)
+            straight[u] = work.tile([P, UNIT_HEADS, PACK, ROTATED], F32, name="straight")
+            crossed[u] = work.tile([P, UNIT_HEADS, PACK, ROTATED], F32, name="crossed")
+            nc.vector.tensor_tensor(
+                out=straight[u][:],
+                in0=r,
+                in1=cos_ps[i][:].unsqueeze(1).to_broadcast([P, UNIT_HEADS, PACK, ROTATED]),
+                op=ALU.mult,
+            )
+            for here, there in ((low, high), (high, low)):
+                nc.vector.tensor_tensor(
+                    out=crossed[u][:, :, :, here],
+                    in0=r[:, :, :, there],
+                    in1=crossed_sin_ps[i][:, :, here].unsqueeze(1).to_broadcast([P, UNIT_HEADS, PACK, HALF]),
+                    op=ALU.mult,
+                )
 
         def combine(u):
-            low, high = slice(0, HALF), slice(HALF, ROTATED)
             nc.gpsimd.tensor_tensor(
-                out=g[u][:, :, :, PLAIN : PLAIN + HALF],
-                in0=r_cos[u][:, :, :, low],
-                in1=r_sin[u][:, :, :, high],
-                op=ALU.add,
-            )
-            nc.gpsimd.tensor_tensor(
-                out=g[u][:, :, :, PLAIN + HALF : HEAD_COLS],
-                in0=r_cos[u][:, :, :, high],
-                in1=r_sin[u][:, :, :, low],
-                op=ALU.subtract,
+                out=g[u][:, :, :, PLAIN:HEAD_COLS], in0=straight[u][:], in1=crossed[u][:], op=ALU.add
             )
 
         def regroup(u):

@@ -29,6 +29,7 @@ UNIT_HEADS = 4
 UNITS_PER_PASS = HEADS // UNIT_HEADS
 UNITS = PASSES * UNITS_PER_PASS
 UNIT_COLS = UNIT_HEADS * HEAD_COLS
+LAST_UNIT = UNITS - 1
 M_TILE = 128
 N_TILE = 512
 M_TILES = HIDDEN // M_TILE
@@ -121,9 +122,8 @@ def tile_gptossmlaattention_pb_k_kernel(tc, hidden_states, cos, sin, Wq, bq, gra
                 )
 
         def combine(u):
-            nc.gpsimd.tensor_tensor(
-                out=g[u][:, :, :, PLAIN:HEAD_COLS], in0=straight[u][:], in1=crossed[u][:], op=ALU.add
-            )
+            adder = nc.vector if u == LAST_UNIT else nc.gpsimd
+            adder.tensor_tensor(out=g[u][:, :, :, PLAIN:HEAD_COLS], in0=straight[u][:], in1=crossed[u][:], op=ALU.add)
 
         def regroup(u):
             i, a = divmod(u, UNITS_PER_PASS)
@@ -131,10 +131,12 @@ def tile_gptossmlaattention_pb_k_kernel(tc, hidden_states, cos, sin, Wq, bq, gra
                 x_grouped[i] = work.tile([P, HIDDEN, PACK], BF16, name="x_grouped", align_bytes=64)
                 nc.scalar.copy(out=x_grouped[i][:], in_=x_raw[i][:].rearrange("p t c -> p c t"))
             dq_grouped[u] = work.tile([P, UNIT_COLS, PACK], BF16, name="dq_grouped", align_bytes=64)
-            nc.scalar.copy(
-                out=dq_grouped[u][:].rearrange("p (h c) t -> p h c t", h=UNIT_HEADS),
-                in_=g[u][:].rearrange("p h t c -> p h c t"),
-            )
+            by_column = dq_grouped[u][:].rearrange("p (h c) t -> p h c t", h=UNIT_HEADS)
+            by_token = g[u][:].rearrange("p h t c -> p h c t")
+            if u == LAST_UNIT:
+                nc.vector.tensor_copy(out=by_column, in_=by_token)
+            else:
+                nc.scalar.copy(out=by_column, in_=by_token)
 
         def quantise(u):
             i, a = divmod(u, UNITS_PER_PASS)
@@ -194,10 +196,11 @@ def tile_gptossmlaattention_pb_k_kernel(tc, hidden_states, cos, sin, Wq, bq, gra
                 quantise(step - 3)
                 contract(step - 3)
 
-        for index, (m, n) in enumerate(sorted(acc)):
-            result = work.tile([M_TILE, N_TILE], F32, name="result", bufs=M_TILES * N_TILES)
-            if index % 2 == 0:
-                nc.vector.tensor_copy(out=result[:], in_=acc[m, n][:])
-            else:
-                nc.scalar.copy(out=result[:], in_=acc[m, n][:])
-            nc.sync.dma_start(out=out[m * M_TILE : (m + 1) * M_TILE, n * N_TILE : (n + 1) * N_TILE], in_=result[:])
+        for n in range(N_TILES):
+            for m in range(M_TILES):
+                result = work.tile([M_TILE, N_TILE], F32, name="result", bufs=M_TILES * N_TILES)
+                if m == 0:
+                    nc.vector.tensor_copy(out=result[:], in_=acc[m, n][:])
+                else:
+                    nc.scalar.copy(out=result[:], in_=acc[m, n][:])
+                nc.sync.dma_start(out=out[m * M_TILE : (m + 1) * M_TILE, n * N_TILE : (n + 1) * N_TILE], in_=result[:])

@@ -19,30 +19,25 @@ TOKENS = 8192
 HIDDEN = 256
 HEADS = 8
 PLAIN = 64
-ROTATED = 128
-HALF = ROTATED // 2
-HEAD_COLS = PLAIN + ROTATED
+ROT = 128
+HALF = ROT // 2
+HEAD_COLS = PLAIN + ROT
 DQ_COLS = HEADS * HEAD_COLS
 
 PASSES = TOKENS // K_PASS
-UNIT_HEADS = 4
-UNITS_PER_PASS = HEADS // UNIT_HEADS
-UNITS = PASSES * UNITS_PER_PASS
-UNIT_COLS = UNIT_HEADS * HEAD_COLS
-LAST_UNIT = UNITS - 1
+SWEEPS = 2
+UNIT_HEADS = HEADS // SWEEPS
+UNITS = SWEEPS * PASSES
+TURNED = 3
+SLOTS = UNITS * TURNED
 M_TILE = 128
 N_TILE = 512
 M_TILES = HIDDEN // M_TILE
-N_TILES = DQ_COLS // N_TILE
+UNIT_PLAIN = UNIT_HEADS * PLAIN
 LOADS_AHEAD = 3
 
 FLOPS = 2 * TOKENS * HIDDEN * DQ_COLS
-BYTES = 2 * TOKENS * (HIDDEN + 2 * ROTATED + DQ_COLS) + 4 * HIDDEN * DQ_COLS
-
-
-def column_cuts(first, last):
-    inner = [c for c in range(first + 1, last) if c % N_TILE == 0]
-    return [first] + inner + [last]
+BYTES = 2 * TOKENS * (HIDDEN + 2 * ROT + DQ_COLS) + 4 * HIDDEN * DQ_COLS
 
 
 def tile_gptossmlaattention_pb_k_kernel(tc, hidden_states, cos, sin, Wq, bq, grad_out, out):
@@ -51,156 +46,236 @@ def tile_gptossmlaattention_pb_k_kernel(tc, hidden_states, cos, sin, Wq, bq, gra
         const = stack.enter_context(tc.tile_pool(name="const", bufs=1))
         loads = stack.enter_context(tc.tile_pool(name="loads", bufs=3))
         work = stack.enter_context(tc.tile_pool(name="work", bufs=3))
-        tables_psum = stack.enter_context(tc.psum_pool(name="tables_psum", bufs=1))
-        acc_psum = stack.enter_context(tc.psum_pool(name="acc_psum", bufs=1))
+        psum = stack.enter_context(tc.psum_pool(name="psum", bufs=1))
         stack.enter_context(tc.manual_schedule())
 
-        identity = const.tile([P, P], BF16, name="identity")
-        make_identity(nc, identity[:])
-        minus_identity = const.tile([P, P], BF16, name="minus_identity")
-        nc.vector.tensor_scalar_mul(out=minus_identity[:], in0=identity[:], scalar1=-1.0)
+        ident = const.tile([P, P], BF16, name="ident")
+        make_identity(nc, ident[:])
+        ident32 = const.tile([P, P], F32, name="ident32")
+        make_identity(nc, ident32[:])
+        swap32 = const.tile([P, P], F32, name="swap32")
+        nc.vector.tensor_copy(out=swap32[:, 0:HALF], in_=ident32[:, HALF:ROT])
+        nc.vector.tensor_copy(out=swap32[:, HALF:ROT], in_=ident32[:, 0:HALF])
 
+        tables, turned, tables_ps = {}, {}, {}
+        g, x_raw = {}, {}
+        r_ps, prods, dq_ps, prods_g = {}, {}, {}, {}
+        x_grouped, plain_grouped, rot_grouped = {}, {}, {}
+        x_codes, x_scales, plain_codes, plain_scales, rot_codes, rot_scales = {}, {}, {}, {}, {}, {}
         acc = {}
-        for m in range(M_TILES):
-            for n in range(N_TILES):
-                acc[m, n] = acc_psum.tile([M_TILE, N_TILE], F32, name="acc_%d_%d" % (m, n))
-
-        cos_sb, sin_sb, x_raw = {}, {}, {}
-        cos_ps, crossed_sin_ps = {}, {}
-        g = {}
-        straight, crossed = {}, {}
-        x_grouped, dq_grouped = {}, {}
-        x_codes, x_scales, dq_codes, dq_scales = {}, {}, {}, {}
 
         def load(u):
-            i, a = divmod(u, UNITS_PER_PASS)
+            s, i = divmod(u, PASSES)
             tokens = slice(i * K_PASS, (i + 1) * K_PASS)
-            if a == 0:
-                cos_sb[i] = loads.tile([P, PACK, ROTATED], BF16, name="cos_sb")
-                sin_sb[i] = loads.tile([P, PACK, ROTATED], BF16, name="sin_sb")
-                nc.sync.dma_start(out=cos_sb[i][:], in_=cos[0, tokens, :].rearrange("(p t) j -> p t j", t=PACK))
-                nc.sync.dma_start(out=sin_sb[i][:], in_=sin[0, tokens, :].rearrange("(p t) j -> p t j", t=PACK))
-            heads = slice(a * UNIT_HEADS, (a + 1) * UNIT_HEADS)
-            g[u] = loads.tile([P, UNIT_HEADS, PACK, HEAD_COLS], BF16, name="g", bufs=LOADS_AHEAD + 3)
-            nc.sync.dma_start(out=g[u][:], in_=grad_out[0, heads, tokens, :].rearrange("h (p t) c -> p h t c", t=PACK))
-            if a == 0:
+            if s == 0:
+                tables[i] = const.tile([P, 2, PACK, ROT], BF16, name="tables_%d" % i)
+                for w, table in ((1, sin), (0, cos)):
+                    nc.sync.dma_start(
+                        out=tables[i][:, w, :, :], in_=table[0, tokens, :].rearrange("(p t) j -> p t j", t=PACK)
+                    )
+            g[u] = loads.tile([P, UNIT_HEADS, PACK, HEAD_COLS], BF16, name="g", bufs=LOADS_AHEAD + 2)
+            for h0, h1 in ((0, 1), (1, 4)) if u == 0 else ((0, 4),):
+                heads = slice(s * UNIT_HEADS + h0, s * UNIT_HEADS + h1)
+                nc.sync.dma_start(
+                    out=g[u][:, h0:h1, :, :], in_=grad_out[0, heads, tokens, :].rearrange("h (p t) c -> p h t c", t=PACK)
+                )
+            if s == 0:
                 x_raw[i] = loads.tile([P, PACK, HIDDEN], BF16, name="x_raw")
                 nc.sync.dma_start(
                     out=x_raw[i][:], in_=hidden_states[0, tokens, :].rearrange("(p t) c -> p t c", t=PACK)
                 )
 
-        low, high = slice(0, HALF), slice(HALF, ROTATED)
+        def negate(i):
+            engine = nc.vector if i == 0 else nc.gpsimd
+            low = tables[i][:, 1, :, 0:HALF]
+            engine.tensor_scalar(out=low, in0=low, scalar1=-1.0, scalar2=0.0, op0=ALU.mult, op1=ALU.add)
 
-        def stage_tables(i):
-            cos_ps[i] = tables_psum.tile([P, PACK, ROTATED], F32, name="cos_ps")
-            crossed_sin_ps[i] = tables_psum.tile([P, PACK, ROTATED], F32, name="crossed_sin_ps")
-            nc.tensor.matmul(out=cos_ps[i][:], lhsT=identity[:], rhs=cos_sb[i][:], start=True, stop=True)
-            nc.tensor.matmul(
-                out=crossed_sin_ps[i][:, :, low], lhsT=identity[:], rhs=sin_sb[i][:, :, high], start=True, stop=True
-            )
-            nc.tensor.matmul(
-                out=crossed_sin_ps[i][:, :, high], lhsT=minus_identity[:], rhs=sin_sb[i][:, :, low], start=True, stop=True
-            )
+        def turn_tables(i):
+            tables_ps[i] = psum.tile([P, 2, PACK, P], BF16, name="tables_ps", tag="bank_%d" % (i % 2))
+            for w in (0, 1):
+                for t in range(PACK):
+                    nc.tensor.transpose(out=tables_ps[i][:, w, t, :], in_=tables[i][:, w, t, :], identity=ident[:])
 
-        def multiply(u):
-            i = u // UNITS_PER_PASS
-            r = g[u][:, :, :, PLAIN:HEAD_COLS]
-            straight[u] = work.tile([P, UNIT_HEADS, PACK, ROTATED], F32, name="straight")
-            crossed[u] = work.tile([P, UNIT_HEADS, PACK, ROTATED], F32, name="crossed")
+        def copy_tables(i):
+            turned[i] = const.tile([P, 2, PACK, P], BF16, name="turned_%d" % i)
+            nc.scalar.copy(out=turned[i][:], in_=tables_ps[i][:])
+
+        def turn(q):
+            u, h = divmod(q, TURNED)
+            r_ps[q] = psum.tile([P, 2 * PACK, P], BF16, name="r_ps", bufs=2)
+            for t in range(PACK):
+                nc.tensor.transpose(out=r_ps[q][:, t, :], in_=g[u][:, h, t, PLAIN:HEAD_COLS], identity=ident[:])
+
+        def multiply(q):
+            i = (q // TURNED) % PASSES
+            prods[q] = work.tile([P, 2, PACK, P], F32, name="prods")
             nc.vector.tensor_tensor(
-                out=straight[u][:],
-                in0=r,
-                in1=cos_ps[i][:].unsqueeze(1).to_broadcast([P, UNIT_HEADS, PACK, ROTATED]),
+                out=prods[q][:],
+                in0=r_ps[q][:, 0:PACK, :].unsqueeze(1).to_broadcast([P, 2, PACK, P]),
+                in1=turned[i][:],
                 op=ALU.mult,
             )
-            for here, there in ((low, high), (high, low)):
-                nc.vector.tensor_tensor(
-                    out=crossed[u][:, :, :, here],
-                    in0=r[:, :, :, there],
-                    in1=crossed_sin_ps[i][:, :, here].unsqueeze(1).to_broadcast([P, UNIT_HEADS, PACK, HALF]),
-                    op=ALU.mult,
-                )
 
-        def combine(u):
-            adder = nc.vector if u == LAST_UNIT else nc.gpsimd
-            adder.tensor_tensor(out=g[u][:, :, :, PLAIN:HEAD_COLS], in0=straight[u][:], in1=crossed[u][:], op=ALU.add)
-
-        def regroup(u):
-            i, a = divmod(u, UNITS_PER_PASS)
-            if a == 0:
-                x_grouped[i] = work.tile([P, HIDDEN, PACK], BF16, name="x_grouped", align_bytes=64)
-                nc.scalar.copy(out=x_grouped[i][:], in_=x_raw[i][:].rearrange("p t c -> p c t"))
-            dq_grouped[u] = work.tile([P, UNIT_COLS, PACK], BF16, name="dq_grouped", align_bytes=64)
-            by_column = dq_grouped[u][:].rearrange("p (h c) t -> p h c t", h=UNIT_HEADS)
-            by_token = g[u][:].rearrange("p h t c -> p h c t")
-            if u == LAST_UNIT:
-                nc.vector.tensor_copy(out=by_column, in_=by_token)
-            else:
-                nc.scalar.copy(out=by_column, in_=by_token)
-
-        def quantise(u):
-            i, a = divmod(u, UNITS_PER_PASS)
-            if a == 0:
-                x_codes[i] = work.tile([P, HIDDEN], U32, name="x_codes", align_bytes=64)
-                x_scales[i] = work.tile([P, HIDDEN], U8, name="x_scales", align_bytes=64)
-                dq_codes[i] = work.tile([P, DQ_COLS], U32, name="dq_codes", align_bytes=64)
-                dq_scales[i] = work.tile([P, DQ_COLS], U8, name="dq_scales", align_bytes=64)
-                nc.vector.quantize_mx(
-                    out=x_codes[i][:].bitcast(E4M3_X4),
-                    scales=x_scales[i][:],
-                    in_=x_grouped[i][:].rearrange("p c t -> p (c t)"),
-                )
-            first = a * UNIT_COLS
-            cuts = column_cuts(first, first + UNIT_COLS)
-            for lo, hi in zip(cuts[:-1], cuts[1:]):
-                nc.vector.quantize_mx(
-                    out=dq_codes[i][:, lo:hi].bitcast(E5M2_X4),
-                    scales=dq_scales[i][:, lo:hi],
-                    in_=dq_grouped[u][:, lo - first : hi - first, :].rearrange("p c t -> p (c t)"),
-                )
-
-        def contract(u):
-            i, a = divmod(u, UNITS_PER_PASS)
-            first = a * UNIT_COLS
-            for n in range(N_TILES):
-                if not first < (n + 1) * N_TILE <= first + UNIT_COLS:
-                    continue
-                n_cols = slice(n * N_TILE, (n + 1) * N_TILE)
-                for m in range(M_TILES):
-                    m_cols = slice(m * M_TILE, (m + 1) * M_TILE)
-                    nc.tensor.matmul_mx(
-                        out=acc[m, n][:],
-                        lhsT=x_codes[i][:, m_cols].bitcast(E4M3_X4),
-                        lhsT_scale=x_scales[i][:, m_cols],
-                        rhs=dq_codes[i][:, n_cols].bitcast(E5M2_X4),
-                        rhs_scale=dq_scales[i][:, n_cols],
-                        start=(i == 0),
-                        stop=(i == PASSES - 1),
+        def add(q):
+            dq_ps[q] = psum.tile([P, PACK, ROT], F32, name="dq_ps", bufs=2)
+            for t in range(PACK):
+                for w, order in ((0, ident32), (1, swap32)):
+                    nc.tensor.matmul(
+                        out=dq_ps[q][:, t, :],
+                        lhsT=prods[q][:, w, t, :],
+                        rhs=order[:],
+                        start=(w == 0),
+                        stop=(w == 1),
+                        is_transpose=True,
                     )
+
+        def round_off(q):
+            u, h = divmod(q, TURNED)
+            if h == 0:
+                rot_grouped[u] = work.tile([P, N_TILE, PACK], BF16, name="rot_grouped", align_bytes=64)
+            nc.scalar.copy(
+                out=rot_grouped[u][:, h * ROT : (h + 1) * ROT, :], in_=dq_ps[q][:].rearrange("p t j -> p j t")
+            )
+
+        def multiply_g(u):
+            i = u % PASSES
+            prods_g[u] = work.tile([P, 2, PACK, ROT], F32, name="prods_g", bufs=2)
+            nc.gpsimd.tensor_tensor(
+                out=prods_g[u][:],
+                in0=g[u][:, TURNED, :, PLAIN:HEAD_COLS].unsqueeze(1).to_broadcast([P, 2, PACK, ROT]),
+                in1=tables[i][:],
+                op=ALU.mult,
+            )
+
+        def add_g(u):
+            straight = prods_g[u][:, 0, :, :].rearrange("p t (x j) -> p x j t", x=2)
+            crossed = prods_g[u][:, 1, :, :].rearrange("p t (x j) -> p x j t", x=2)
+            nc.gpsimd.tensor_tensor(
+                out=rot_grouped[u][:, TURNED * ROT :, :].rearrange("p (x j) t -> p x j t", x=2),
+                in0=straight,
+                in1=crossed[:, ::-1, :, :],
+                op=ALU.add,
+            )
+
+        def regroup_plain(u):
+            plain_grouped[u] = work.tile([P, UNIT_PLAIN, PACK], BF16, name="plain_grouped", align_bytes=64)
+            nc.scalar.copy(
+                out=plain_grouped[u][:].rearrange("p (h c) t -> p h c t", h=UNIT_HEADS),
+                in_=g[u][:, :, :, 0:PLAIN].rearrange("p h t c -> p h c t"),
+            )
+
+        def regroup_x(i):
+            x_grouped[i] = work.tile([P, HIDDEN, PACK], BF16, name="x_grouped", align_bytes=64)
+            nc.scalar.copy(out=x_grouped[i][:], in_=x_raw[i][:].rearrange("p t c -> p c t"))
+
+        def quantise_x(i):
+            x_codes[i] = const.tile([P, HIDDEN], U32, name="x_codes_%d" % i, align_bytes=64)
+            x_scales[i] = const.tile([P, HIDDEN], U8, name="x_scales_%d" % i, align_bytes=64)
+            nc.vector.quantize_mx(
+                out=x_codes[i][:].bitcast(E4M3_X4),
+                scales=x_scales[i][:],
+                in_=x_grouped[i][:].rearrange("p c t -> p (c t)"),
+            )
+
+        def quantise_plain(u):
+            s, i = divmod(u, PASSES)
+            if s == 0:
+                plain_codes[i] = const.tile([P, N_TILE], U32, name="plain_codes_%d" % i, align_bytes=64)
+                plain_scales[i] = const.tile([P, N_TILE], U8, name="plain_scales_%d" % i, align_bytes=64)
+            cols = slice(s * UNIT_PLAIN, (s + 1) * UNIT_PLAIN)
+            nc.vector.quantize_mx(
+                out=plain_codes[i][:, cols].bitcast(E5M2_X4),
+                scales=plain_scales[i][:, cols],
+                in_=plain_grouped[u][:].rearrange("p c t -> p (c t)"),
+            )
+
+        def quantise_rot(u):
+            rot_codes[u] = work.tile([P, N_TILE], U32, name="rot_codes", align_bytes=64)
+            rot_scales[u] = work.tile([P, N_TILE], U8, name="rot_scales", align_bytes=64)
+            nc.vector.quantize_mx(
+                out=rot_codes[u][:].bitcast(E5M2_X4),
+                scales=rot_scales[u][:],
+                in_=rot_grouped[u][:].rearrange("p c t -> p (c t)"),
+            )
+
+        def contract(group, i, codes, scales):
+            for m in range(M_TILES):
+                if i == 0:
+                    bank = m if group == 1 else M_TILES + m
+                    acc[group, m] = psum.tile([M_TILE, N_TILE], F32, name="acc", tag="bank_%d" % bank)
+                m_cols = slice(m * M_TILE, (m + 1) * M_TILE)
+                nc.tensor.matmul_mx(
+                    out=acc[group, m][:],
+                    lhsT=x_codes[i][:, m_cols].bitcast(E4M3_X4),
+                    lhsT_scale=x_scales[i][:, m_cols],
+                    rhs=codes[:].bitcast(E5M2_X4),
+                    rhs_scale=scales[:],
+                    start=(i == 0),
+                    stop=(i == PASSES - 1),
+                )
+
+        def store(group, m, copy):
+            result = work.tile([M_TILE, N_TILE], F32, name="result", bufs=4)
+            copy(out=result[:], in_=acc[group, m][:])
+            by_head = out[m * M_TILE : (m + 1) * M_TILE, :].rearrange("m (h c) -> m h c", h=HEADS)
+            if group == 2:
+                to, heads = by_head[:, :, 0:PLAIN], HEADS
+            else:
+                to, heads = by_head[:, group * UNIT_HEADS : (group + 1) * UNIT_HEADS, PLAIN:HEAD_COLS], UNIT_HEADS
+            nc.sync.dma_start(out=to, in_=result[:].rearrange("m (h c) -> m h c", h=heads))
 
         for u in range(LOADS_AHEAD):
             load(u)
-        stage_tables(0)
-        for step in range(UNITS + 3):
-            if step + LOADS_AHEAD < UNITS:
-                load(step + LOADS_AHEAD)
-            if step < UNITS:
-                multiply(step)
-                if (step + 1) % UNITS_PER_PASS == 0 and step + 1 < UNITS:
-                    stage_tables((step + 1) // UNITS_PER_PASS)
-            if 0 <= step - 1 < UNITS:
-                combine(step - 1)
-            if 0 <= step - 2 < UNITS:
-                regroup(step - 2)
-            if 0 <= step - 3:
-                quantise(step - 3)
-                contract(step - 3)
+        negate(0)
+        turn_tables(0)
+        copy_tables(0)
+        negate(1)
+        turn(0)
+        for q in range(SLOTS + 2 * TURNED):
+            u, phase = divmod(q, TURNED)
+            if phase == 0 and u + LOADS_AHEAD < UNITS:
+                load(u + LOADS_AHEAD)
+            if q + 1 < SLOTS:
+                turn(q + 1)
+            if q < SLOTS:
+                multiply(q)
+            if 0 <= q - 1 < SLOTS:
+                add(q - 1)
+            if 0 <= q - 2 < SLOTS:
+                round_off(q - 2)
+            if phase == 0:
+                if u + 2 < PASSES:
+                    negate(u + 2)
+                if u + 1 < PASSES:
+                    turn_tables(u + 1)
+                if u < UNITS:
+                    multiply_g(u)
+                if 0 <= u - 1 < UNITS:
+                    quantise_plain(u - 1)
+                if 0 <= u - 2 < UNITS:
+                    s, i = divmod(u - 2, PASSES)
+                    if s == 1:
+                        contract(2, i, plain_codes[i], plain_scales[i])
+                    contract(s, i, rot_codes[u - 2], rot_scales[u - 2])
+            if phase == 1:
+                if u + 1 < PASSES:
+                    copy_tables(u + 1)
+                if u < UNITS:
+                    regroup_plain(u)
+                if 0 <= u - 1 < PASSES:
+                    quantise_x(u - 1)
+                if u == PASSES + 1:
+                    store(0, 0, nc.scalar.copy)
+            if phase == 2:
+                if u < UNITS:
+                    add_g(u)
+                if u < PASSES:
+                    regroup_x(u)
+                if 0 <= u - 1 < UNITS:
+                    quantise_rot(u - 1)
+                if u == PASSES + 1:
+                    store(0, 1, nc.scalar.copy)
 
-        for n in range(N_TILES):
-            for m in range(M_TILES):
-                result = work.tile([M_TILE, N_TILE], F32, name="result", bufs=M_TILES * N_TILES)
-                if m == 0:
-                    nc.vector.tensor_copy(out=result[:], in_=acc[m, n][:])
-                else:
-                    nc.scalar.copy(out=result[:], in_=acc[m, n][:])
-                nc.sync.dma_start(out=out[m * M_TILE : (m + 1) * M_TILE, n * N_TILE : (n + 1) * N_TILE], in_=result[:])
+        for group in (2, 1):
+            store(group, 0, nc.vector.tensor_copy)
+            store(group, 1, nc.scalar.copy)

@@ -116,8 +116,16 @@ def tile_gptossmlaattention_pb_k_kernel(tc, hidden_states, cos, sin, Wq, bq, gra
                 op=ALU.mult,
             )
 
+        def keep_warm(bank):
+            nc.tensor.matmul(
+                out=bank[:], lhsT=ident[:], rhs=ident[:].unsqueeze(1).to_broadcast([P, PACK, P]), start=True, stop=True
+            )
+
         def add(q):
+            u, phase = divmod(q + 1, TURNED)
             dq_ps[q] = psum.tile([P, PACK, ROT], F32, name="dq_ps", bufs=2)
+            if u < PASSES and phase > 0:
+                keep_warm(dq_ps[q])
             for t in range(PACK):
                 for w, order in ((0, ident32), (1, swap32)):
                     nc.tensor.matmul(
@@ -198,8 +206,8 @@ def tile_gptossmlaattention_pb_k_kernel(tc, hidden_states, cos, sin, Wq, bq, gra
                 in_=rot_grouped[u][:].rearrange("p c t -> p (c t)"),
             )
 
-        def contract(group, i, codes, scales):
-            for m in range(M_TILES):
+        def contract(group, i, codes, scales, ms=(0, 1)):
+            for m in ms:
                 if i == 0:
                     bank = m if group == 1 else M_TILES + m
                     acc[group, m] = psum.tile([M_TILE, N_TILE], F32, name="acc", tag="bank_%d" % bank)
@@ -226,12 +234,15 @@ def tile_gptossmlaattention_pb_k_kernel(tc, hidden_states, cos, sin, Wq, bq, gra
 
         for u in range(LOADS_AHEAD):
             load(u)
+        warm = psum.tile([P, PACK, ROT], F32, name="dq_ps", bufs=2)
+        for i in range(6):
+            keep_warm(warm)
         negate(0)
         turn_tables(0)
         copy_tables(0)
         negate(1)
         turn(0)
-        for q in range(SLOTS + 2 * TURNED):
+        for q in range(SLOTS + 3 * TURNED):
             u, phase = divmod(q, TURNED)
             if phase == 0 and u + LOADS_AHEAD < UNITS:
                 load(u + LOADS_AHEAD)
@@ -256,7 +267,14 @@ def tile_gptossmlaattention_pb_k_kernel(tc, hidden_states, cos, sin, Wq, bq, gra
                     s, i = divmod(u - 2, PASSES)
                     if s == 1:
                         contract(2, i, plain_codes[i], plain_scales[i])
-                    contract(s, i, rot_codes[u - 2], rot_scales[u - 2])
+                    else:
+                        contract(0, i, rot_codes[u - 2], rot_scales[u - 2], (0,))
+            if phase > 0 and 0 <= u - 2 < UNITS:
+                s, i = divmod(u - 2, PASSES)
+                if s == 1:
+                    contract(1, i, rot_codes[u - 2], rot_scales[u - 2], (phase - 1,))
+                elif phase == 1:
+                    contract(0, i, rot_codes[u - 2], rot_scales[u - 2], (1,))
             if phase == 1:
                 if u + 1 < PASSES:
                     copy_tables(u + 1)

@@ -86,9 +86,8 @@ def tile_gptossmlaattention_pb_k_kernel(tc, hidden_states, cos, sin, Wq, bq, gra
                 )
 
         def negate(i):
-            engine = nc.vector if i == 0 else nc.gpsimd
             low = tables[i][:, 1, :, 0:HALF]
-            engine.tensor_scalar(out=low, in0=low, scalar1=-1.0, scalar2=0.0, op0=ALU.mult, op1=ALU.add)
+            nc.vector.tensor_scalar(out=low, in0=low, scalar1=-1.0, scalar2=0.0, op0=ALU.mult, op1=ALU.add)
 
         def turn_tables(i):
             tables_ps[i] = psum.tile([P, 2, PACK, P], BF16, name="tables_ps", tag="bank_%d" % (i % 2))
@@ -139,8 +138,6 @@ def tile_gptossmlaattention_pb_k_kernel(tc, hidden_states, cos, sin, Wq, bq, gra
 
         def round_off(q):
             u, h = divmod(q, TURNED)
-            if h == 0:
-                rot_grouped[u] = work.tile([P, N_TILE, PACK], BF16, name="rot_grouped", align_bytes=64)
             nc.scalar.copy(
                 out=rot_grouped[u][:, h * ROT : (h + 1) * ROT, :], in_=dq_ps[q][:].rearrange("p t j -> p j t")
             )
@@ -156,6 +153,7 @@ def tile_gptossmlaattention_pb_k_kernel(tc, hidden_states, cos, sin, Wq, bq, gra
             )
 
         def add_g(u):
+            rot_grouped[u] = work.tile([P, N_TILE, PACK], BF16, name="rot_grouped", align_bytes=64, bufs=2)
             straight = prods_g[u][:, 0, :, :].rearrange("p t (x j) -> p x j t", x=2)
             crossed = prods_g[u][:, 1, :, :].rearrange("p t (x j) -> p x j t", x=2)
             nc.gpsimd.tensor_tensor(
@@ -242,10 +240,15 @@ def tile_gptossmlaattention_pb_k_kernel(tc, hidden_states, cos, sin, Wq, bq, gra
         copy_tables(0)
         negate(1)
         turn(0)
+        multiply_g(0)
         for q in range(SLOTS + 3 * TURNED):
             u, phase = divmod(q, TURNED)
             if phase == 0 and u + LOADS_AHEAD < UNITS:
                 load(u + LOADS_AHEAD)
+            if phase == 0 and u < UNITS:
+                add_g(u)
+                if u + 1 < UNITS:
+                    multiply_g(u + 1)
             if q + 1 < SLOTS:
                 turn(q + 1)
             if q < SLOTS:
@@ -255,14 +258,8 @@ def tile_gptossmlaattention_pb_k_kernel(tc, hidden_states, cos, sin, Wq, bq, gra
             if 0 <= q - 2 < SLOTS:
                 round_off(q - 2)
             if phase == 0:
-                if u + 2 < PASSES:
-                    negate(u + 2)
                 if u + 1 < PASSES:
                     turn_tables(u + 1)
-                if u < UNITS:
-                    multiply_g(u)
-                if 0 <= u - 1 < UNITS:
-                    quantise_plain(u - 1)
                 if 0 <= u - 2 < UNITS:
                     s, i = divmod(u - 2, PASSES)
                     if s == 1:
@@ -280,16 +277,17 @@ def tile_gptossmlaattention_pb_k_kernel(tc, hidden_states, cos, sin, Wq, bq, gra
                     copy_tables(u + 1)
                 if u < UNITS:
                     regroup_plain(u)
-                if 0 <= u - 1 < PASSES:
-                    quantise_x(u - 1)
                 if u == PASSES + 1:
                     store(0, 0, nc.scalar.copy)
             if phase == 2:
-                if u < UNITS:
-                    add_g(u)
                 if u < PASSES:
                     regroup_x(u)
+                if u + 2 < PASSES:
+                    negate(u + 2)
+                if 0 <= u - 1 < PASSES:
+                    quantise_x(u - 1)
                 if 0 <= u - 1 < UNITS:
+                    quantise_plain(u - 1)
                     quantise_rot(u - 1)
                 if u == PASSES + 1:
                     store(0, 1, nc.scalar.copy)

@@ -59,7 +59,7 @@ def tile_gptossmlaattention_pb_k_kernel(tc, hidden_states, cos, sin, Wq, bq, gra
 
         tables, turned, tables_ps = {}, {}, {}
         g, x_raw = {}, {}
-        r_ps, prods, dq_ps, prods_g = {}, {}, {}, {}
+        r_ps, prods, dq_ps, prods_g, sums_g = {}, {}, {}, {}, {}
         x_grouped, plain_grouped, rot_grouped = {}, {}, {}
         x_codes, x_scales, plain_codes, plain_scales, rot_codes, rot_scales = {}, {}, {}, {}, {}, {}
         acc = {}
@@ -120,11 +120,10 @@ def tile_gptossmlaattention_pb_k_kernel(tc, hidden_states, cos, sin, Wq, bq, gra
                 out=bank[:], lhsT=ident[:], rhs=ident[:].unsqueeze(1).to_broadcast([P, PACK, P]), start=True, stop=True
             )
 
-        def add(q):
-            u, phase = divmod(q + 1, TURNED)
+        def open_bank(q):
             dq_ps[q] = psum.tile([P, PACK, ROT], F32, name="dq_ps", bufs=2)
-            if u < PASSES and phase > 0:
-                keep_warm(dq_ps[q])
+
+        def add(q):
             for t in range(PACK):
                 for w, order in ((0, ident32), (1, swap32)):
                     nc.tensor.matmul(
@@ -153,26 +152,35 @@ def tile_gptossmlaattention_pb_k_kernel(tc, hidden_states, cos, sin, Wq, bq, gra
             )
 
         def add_g(u):
-            rot_grouped[u] = work.tile([P, N_TILE, PACK], BF16, name="rot_grouped", align_bytes=64, bufs=2)
-            straight = prods_g[u][:, 0, :, :].rearrange("p t (x j) -> p x j t", x=2)
-            crossed = prods_g[u][:, 1, :, :].rearrange("p t (x j) -> p x j t", x=2)
+            rot_grouped[u] = work.tile([P, N_TILE + ROT, PACK], BF16, name="rot_grouped", align_bytes=64, bufs=2)
+            sums_g[u] = rot_grouped[u][:, N_TILE:, :].rearrange("p c t -> p (c t)")
             nc.gpsimd.tensor_tensor(
-                out=rot_grouped[u][:, TURNED * ROT :, :].rearrange("p (x j) t -> p x j t", x=2),
-                in0=straight,
-                in1=crossed[:, ::-1, :, :],
+                out=sums_g[u].rearrange("p (t x j) -> p t x j", t=PACK, x=2),
+                in0=prods_g[u][:, 0, :, :].rearrange("p t (x j) -> p t x j", x=2),
+                in1=prods_g[u][:, 1, :, :].rearrange("p t (x j) -> p t x j", x=2)[:, :, ::-1, :],
                 op=ALU.add,
+            )
+
+        def regroup_g(u):
+            by_column(
+                rot_grouped[u][:, TURNED * ROT : N_TILE, :], sums_g[u].rearrange("p (t c) -> p t c", t=PACK)
+            )
+
+        def by_column(grouped, rows):
+            nc.scalar.copy(
+                out=grouped.rearrange("p (c i) t -> p c t i", i=4), in_=rows.rearrange("p t (c i) -> p c t i", i=4)
             )
 
         def regroup_plain(u):
             plain_grouped[u] = work.tile([P, UNIT_PLAIN, PACK], BF16, name="plain_grouped", align_bytes=64)
             nc.scalar.copy(
-                out=plain_grouped[u][:].rearrange("p (h c) t -> p h c t", h=UNIT_HEADS),
-                in_=g[u][:, :, :, 0:PLAIN].rearrange("p h t c -> p h c t"),
+                out=plain_grouped[u][:].rearrange("p (h c i) t -> p h c t i", h=UNIT_HEADS, i=4),
+                in_=g[u][:, :, :, 0:PLAIN].rearrange("p h t (c i) -> p h c t i", i=4),
             )
 
         def regroup_x(i):
             x_grouped[i] = work.tile([P, HIDDEN, PACK], BF16, name="x_grouped", align_bytes=64)
-            nc.scalar.copy(out=x_grouped[i][:], in_=x_raw[i][:].rearrange("p t c -> p c t"))
+            by_column(x_grouped[i][:], x_raw[i][:])
 
         def quantise_x(i):
             x_codes[i] = const.tile([P, HIDDEN], U32, name="x_codes_%d" % i, align_bytes=64)
@@ -201,11 +209,11 @@ def tile_gptossmlaattention_pb_k_kernel(tc, hidden_states, cos, sin, Wq, bq, gra
             nc.vector.quantize_mx(
                 out=rot_codes[u][:].bitcast(E5M2_X4),
                 scales=rot_scales[u][:],
-                in_=rot_grouped[u][:].rearrange("p c t -> p (c t)"),
+                in_=rot_grouped[u][:, 0:N_TILE, :].rearrange("p c t -> p (c t)"),
             )
 
-        def contract(group, i, codes, scales, ms=(0, 1)):
-            for m in ms:
+        def contract(group, i, codes, scales):
+            for m in range(M_TILES):
                 if i == 0:
                     bank = m if group == 1 else M_TILES + m
                     acc[group, m] = psum.tile([M_TILE, N_TILE], F32, name="acc", tag="bank_%d" % bank)
@@ -241,7 +249,7 @@ def tile_gptossmlaattention_pb_k_kernel(tc, hidden_states, cos, sin, Wq, bq, gra
         negate(1)
         turn(0)
         multiply_g(0)
-        for q in range(SLOTS + 3 * TURNED):
+        for q in range(SLOTS + 2 * TURNED):
             u, phase = divmod(q, TURNED)
             if phase == 0 and u + LOADS_AHEAD < UNITS:
                 load(u + LOADS_AHEAD)
@@ -254,24 +262,23 @@ def tile_gptossmlaattention_pb_k_kernel(tc, hidden_states, cos, sin, Wq, bq, gra
             if q < SLOTS:
                 multiply(q)
             if 0 <= q - 1 < SLOTS:
+                open_bank(q - 1)
+            if phase == 0:
+                if 0 < u <= PASSES:
+                    keep_warm(dq_ps[q - 1])
+                    keep_warm(dq_ps[q - 1])
+                if 0 <= u - 2 < UNITS:
+                    s, i = divmod(u - 2, PASSES)
+                    if s == 1:
+                        contract(2, i, plain_codes[i], plain_scales[i])
+                    contract(s, i, rot_codes[u - 2], rot_scales[u - 2])
+            if 0 <= q - 1 < SLOTS:
                 add(q - 1)
             if 0 <= q - 2 < SLOTS:
                 round_off(q - 2)
             if phase == 0:
                 if u + 1 < PASSES:
                     turn_tables(u + 1)
-                if 0 <= u - 2 < UNITS:
-                    s, i = divmod(u - 2, PASSES)
-                    if s == 1:
-                        contract(2, i, plain_codes[i], plain_scales[i])
-                    else:
-                        contract(0, i, rot_codes[u - 2], rot_scales[u - 2], (0,))
-            if phase > 0 and 0 <= u - 2 < UNITS:
-                s, i = divmod(u - 2, PASSES)
-                if s == 1:
-                    contract(1, i, rot_codes[u - 2], rot_scales[u - 2], (phase - 1,))
-                elif phase == 1:
-                    contract(0, i, rot_codes[u - 2], rot_scales[u - 2], (1,))
             if phase == 1:
                 if u + 1 < PASSES:
                     copy_tables(u + 1)
@@ -280,6 +287,8 @@ def tile_gptossmlaattention_pb_k_kernel(tc, hidden_states, cos, sin, Wq, bq, gra
                 if u == PASSES + 1:
                     store(0, 0, nc.scalar.copy)
             if phase == 2:
+                if u < UNITS:
+                    regroup_g(u)
                 if u < PASSES:
                     regroup_x(u)
                 if u + 2 < PASSES:

@@ -58,7 +58,7 @@ def tile_gptossmlaattention_pb_k_kernel(tc, hidden_states, cos, sin, Wq, bq, gra
         nc.vector.tensor_copy(out=swap32[:, HALF:ROT], in_=ident32[:, 0:HALF])
 
         tables, turned, tables_ps = {}, {}, {}
-        g, x_raw = {}, {}
+        g, x_raw, plain_raw = {}, {}, {}
         r_ps, prods, dq_ps, prods_g, sums_g = {}, {}, {}, {}, {}
         x_grouped, plain_grouped, rot_grouped = {}, {}, {}
         x_codes, x_scales, plain_codes, plain_scales, rot_codes, rot_scales = {}, {}, {}, {}, {}, {}
@@ -79,6 +79,13 @@ def tile_gptossmlaattention_pb_k_kernel(tc, hidden_states, cos, sin, Wq, bq, gra
                 nc.sync.dma_start(
                     out=g[u][:, h0:h1, :, :], in_=grad_out[0, heads, tokens, :].rearrange("h (p t) c -> p h t c", t=PACK)
                 )
+            if s == 1:
+                plain_raw[i] = loads.tile([P, UNIT_HEADS, PACK, PLAIN], BF16, name="plain_raw")
+                for h in range(UNIT_HEADS):
+                    nc.sync.dma_start(
+                        out=plain_raw[i][:, h, :, :],
+                        in_=grad_out[0, h, tokens, 0:PLAIN].rearrange("(p t) c -> p t c", t=PACK),
+                    )
             if s == 0:
                 x_raw[i] = loads.tile([P, PACK, HIDDEN], BF16, name="x_raw")
                 nc.sync.dma_start(
@@ -90,7 +97,7 @@ def tile_gptossmlaattention_pb_k_kernel(tc, hidden_states, cos, sin, Wq, bq, gra
             nc.vector.tensor_scalar(out=low, in0=low, scalar1=-1.0, scalar2=0.0, op0=ALU.mult, op1=ALU.add)
 
         def turn_tables(i):
-            tables_ps[i] = psum.tile([P, 2, PACK, P], BF16, name="tables_ps", tag="bank_%d" % (i % 2))
+            tables_ps[i] = psum.tile([P, 2, PACK, P], BF16, name="tables_ps", tag="bank_0")
             for w in (0, 1):
                 for t in range(PACK):
                     nc.tensor.transpose(out=tables_ps[i][:, w, t, :], in_=tables[i][:, w, t, :], identity=ident[:])
@@ -101,16 +108,18 @@ def tile_gptossmlaattention_pb_k_kernel(tc, hidden_states, cos, sin, Wq, bq, gra
 
         def turn(q):
             u, h = divmod(q, TURNED)
-            r_ps[q] = psum.tile([P, 2 * PACK, P], BF16, name="r_ps", bufs=2)
+            if q % 2 == 0:
+                pair = psum.tile([P, 2 * PACK, P], BF16, name="r_ps", bufs=2)
+                r_ps[q], r_ps[q + 1] = pair[:, 0:PACK, :], pair[:, PACK:, :]
             for t in range(PACK):
                 nc.tensor.transpose(out=r_ps[q][:, t, :], in_=g[u][:, h, t, PLAIN:HEAD_COLS], identity=ident[:])
 
         def multiply(q):
             i = (q // TURNED) % PASSES
-            prods[q] = work.tile([P, 2, PACK, P], F32, name="prods")
+            prods[q] = work.tile([P, 2, PACK, P], F32, name="prods", bufs=6)
             nc.vector.tensor_tensor(
                 out=prods[q][:],
-                in0=r_ps[q][:, 0:PACK, :].unsqueeze(1).to_broadcast([P, 2, PACK, P]),
+                in0=r_ps[q].unsqueeze(1).to_broadcast([P, 2, PACK, P]),
                 in1=turned[i][:],
                 op=ALU.mult,
             )
@@ -121,7 +130,8 @@ def tile_gptossmlaattention_pb_k_kernel(tc, hidden_states, cos, sin, Wq, bq, gra
             )
 
         def open_bank(q):
-            dq_ps[q] = psum.tile([P, PACK, ROT], F32, name="dq_ps", bufs=2)
+            banks = ("dq_0", "dq_1", "bank_1") if q < SLOTS // SWEEPS else ("dq_0", "dq_1")
+            dq_ps[q] = psum.tile([P, PACK, ROT], F32, name="dq_ps", tag=banks[q % len(banks)])
 
         def add(q):
             for t in range(PACK):
@@ -152,7 +162,7 @@ def tile_gptossmlaattention_pb_k_kernel(tc, hidden_states, cos, sin, Wq, bq, gra
             )
 
         def add_g(u):
-            rot_grouped[u] = work.tile([P, N_TILE + ROT, PACK], BF16, name="rot_grouped", align_bytes=64, bufs=2)
+            rot_grouped[u] = work.tile([P, N_TILE + ROT, PACK], BF16, name="rot_grouped", align_bytes=64)
             sums_g[u] = rot_grouped[u][:, N_TILE:, :].rearrange("p c t -> p (c t)")
             nc.gpsimd.tensor_tensor(
                 out=sums_g[u].rearrange("p (t x j) -> p t x j", t=PACK, x=2),
@@ -171,11 +181,15 @@ def tile_gptossmlaattention_pb_k_kernel(tc, hidden_states, cos, sin, Wq, bq, gra
                 out=grouped.rearrange("p (c i) t -> p c t i", i=4), in_=rows.rearrange("p t (c i) -> p c t i", i=4)
             )
 
-        def regroup_plain(u):
-            plain_grouped[u] = work.tile([P, UNIT_PLAIN, PACK], BF16, name="plain_grouped", align_bytes=64)
+        def regroup_plain(i, half):
+            if half == 0:
+                plain_grouped[i] = work.tile([P, N_TILE, PACK], BF16, name="plain_grouped", align_bytes=64)
+            source = plain_raw[i][:] if half == 0 else g[PASSES + i][:, :, :, 0:PLAIN]
             nc.scalar.copy(
-                out=plain_grouped[u][:].rearrange("p (h c i) t -> p h c t i", h=UNIT_HEADS, i=4),
-                in_=g[u][:, :, :, 0:PLAIN].rearrange("p h t (c i) -> p h c t i", i=4),
+                out=plain_grouped[i][:, half * UNIT_PLAIN : (half + 1) * UNIT_PLAIN, :].rearrange(
+                    "p (h c i) t -> p h c t i", h=UNIT_HEADS, i=4
+                ),
+                in_=source.rearrange("p h t (c i) -> p h c t i", i=4),
             )
 
         def regroup_x(i):
@@ -191,16 +205,13 @@ def tile_gptossmlaattention_pb_k_kernel(tc, hidden_states, cos, sin, Wq, bq, gra
                 in_=x_grouped[i][:].rearrange("p c t -> p (c t)"),
             )
 
-        def quantise_plain(u):
-            s, i = divmod(u, PASSES)
-            if s == 0:
-                plain_codes[i] = const.tile([P, N_TILE], U32, name="plain_codes_%d" % i, align_bytes=64)
-                plain_scales[i] = const.tile([P, N_TILE], U8, name="plain_scales_%d" % i, align_bytes=64)
-            cols = slice(s * UNIT_PLAIN, (s + 1) * UNIT_PLAIN)
+        def quantise_plain(i):
+            plain_codes[i] = work.tile([P, N_TILE], U32, name="plain_codes", align_bytes=64)
+            plain_scales[i] = work.tile([P, N_TILE], U8, name="plain_scales", align_bytes=64)
             nc.vector.quantize_mx(
-                out=plain_codes[i][:, cols].bitcast(E5M2_X4),
-                scales=plain_scales[i][:, cols],
-                in_=plain_grouped[u][:].rearrange("p c t -> p (c t)"),
+                out=plain_codes[i][:].bitcast(E5M2_X4),
+                scales=plain_scales[i][:],
+                in_=plain_grouped[i][:].rearrange("p c t -> p (c t)"),
             )
 
         def quantise_rot(u):
@@ -240,7 +251,7 @@ def tile_gptossmlaattention_pb_k_kernel(tc, hidden_states, cos, sin, Wq, bq, gra
 
         for u in range(LOADS_AHEAD):
             load(u)
-        warm = psum.tile([P, PACK, ROT], F32, name="dq_ps", bufs=2)
+        warm = psum.tile([P, PACK, ROT], F32, name="warm", tag="dq_0")
         for i in range(6):
             keep_warm(warm)
         negate(0)
@@ -248,57 +259,61 @@ def tile_gptossmlaattention_pb_k_kernel(tc, hidden_states, cos, sin, Wq, bq, gra
         copy_tables(0)
         negate(1)
         turn(0)
+        turn(1)
         multiply_g(0)
-        for q in range(SLOTS + 2 * TURNED):
+        for q in range(SLOTS + 4 * TURNED):
             u, phase = divmod(q, TURNED)
+            first_even = q % 2 == 0 and phase < 2
             if phase == 0 and u + LOADS_AHEAD < UNITS:
                 load(u + LOADS_AHEAD)
             if phase == 0 and u < UNITS:
                 add_g(u)
                 if u + 1 < UNITS:
                     multiply_g(u + 1)
-            if q + 1 < SLOTS:
-                turn(q + 1)
+            if 0 <= q - 3 < SLOTS:
+                round_off(q - 3)
+            if q % 2 == 0:
+                for ahead in (q + 2, q + 3):
+                    if ahead < SLOTS:
+                        turn(ahead)
+                if first_even and u + 1 < PASSES:
+                    turn_tables(u + 1)
+                behind = [b for b in (q - 2, q - 1) if 0 <= b < SLOTS]
+                for b in behind:
+                    open_bank(b)
+                if first_even:
+                    if 0 <= u - 3 < UNITS:
+                        s, i = divmod(u - 3, PASSES)
+                        if s == 1:
+                            contract(2, i, plain_codes[i], plain_scales[i])
+                        contract(s, i, rot_codes[u - 3], rot_scales[u - 3])
+                for b in behind:
+                    add(b)
             if q < SLOTS:
                 multiply(q)
-            if 0 <= q - 1 < SLOTS:
-                open_bank(q - 1)
-            if phase == 0:
-                if 0 < u <= PASSES:
-                    keep_warm(dq_ps[q - 1])
-                    keep_warm(dq_ps[q - 1])
-                if 0 <= u - 2 < UNITS:
-                    s, i = divmod(u - 2, PASSES)
-                    if s == 1:
-                        contract(2, i, plain_codes[i], plain_scales[i])
-                    contract(s, i, rot_codes[u - 2], rot_scales[u - 2])
-            if 0 <= q - 1 < SLOTS:
-                add(q - 1)
-            if 0 <= q - 2 < SLOTS:
-                round_off(q - 2)
-            if phase == 0:
-                if u + 1 < PASSES:
-                    turn_tables(u + 1)
+            if first_even and u + 1 < PASSES:
+                copy_tables(u + 1)
+            if phase == 0 and PASSES <= u < UNITS:
+                regroup_plain(u - PASSES, 0)
             if phase == 1:
-                if u + 1 < PASSES:
-                    copy_tables(u + 1)
-                if u < UNITS:
-                    regroup_plain(u)
-                if u == PASSES + 1:
+                if u < PASSES:
+                    regroup_x(u)
+                elif u < UNITS:
+                    regroup_plain(u - PASSES, 1)
+                if u == PASSES + 2:
                     store(0, 0, nc.scalar.copy)
             if phase == 2:
                 if u < UNITS:
                     regroup_g(u)
-                if u < PASSES:
-                    regroup_x(u)
                 if u + 2 < PASSES:
                     negate(u + 2)
+                if 0 <= u - 2 < UNITS:
+                    quantise_rot(u - 2)
                 if 0 <= u - 1 < PASSES:
                     quantise_x(u - 1)
-                if 0 <= u - 1 < UNITS:
-                    quantise_plain(u - 1)
-                    quantise_rot(u - 1)
-                if u == PASSES + 1:
+                if PASSES <= u - 1 < UNITS:
+                    quantise_plain(u - 1 - PASSES)
+                if u == PASSES + 2:
                     store(0, 1, nc.scalar.copy)
 
         for group in (2, 1):

@@ -223,21 +223,24 @@ def tile_gptossmlaattention_pb_k_kernel(tc, hidden_states, cos, sin, Wq, bq, gra
                 in_=rot_grouped[u][:, 0:N_TILE, :].rearrange("p c t -> p (c t)"),
             )
 
-        def contract(group, i, codes, scales):
-            for m in range(M_TILES):
-                if i == 0:
-                    bank = m if group == 1 else M_TILES + m
-                    acc[group, m] = psum.tile([M_TILE, N_TILE], F32, name="acc", tag="bank_%d" % bank)
-                m_cols = slice(m * M_TILE, (m + 1) * M_TILE)
-                nc.tensor.matmul_mx(
-                    out=acc[group, m][:],
-                    lhsT=x_codes[i][:, m_cols].bitcast(E4M3_X4),
-                    lhsT_scale=x_scales[i][:, m_cols],
-                    rhs=codes[:].bitcast(E5M2_X4),
-                    rhs_scale=scales[:],
-                    start=(i == 0),
-                    stop=(i == PASSES - 1),
-                )
+        def contract(group, i, m):
+            if group == 2:
+                codes, scales = plain_codes[i], plain_scales[i]
+            else:
+                codes, scales = rot_codes[group * PASSES + i], rot_scales[group * PASSES + i]
+            if i == 0:
+                bank = m if group == 1 else M_TILES + m
+                acc[group, m] = psum.tile([M_TILE, N_TILE], F32, name="acc", tag="bank_%d" % bank)
+            m_cols = slice(m * M_TILE, (m + 1) * M_TILE)
+            nc.tensor.matmul_mx(
+                out=acc[group, m][:],
+                lhsT=x_codes[i][:, m_cols].bitcast(E4M3_X4),
+                lhsT_scale=x_scales[i][:, m_cols],
+                rhs=codes[:].bitcast(E5M2_X4),
+                rhs_scale=scales[:],
+                start=(i == 0),
+                stop=(i == PASSES - 1),
+            )
 
         def store(group, m, copy):
             result = work.tile([M_TILE, N_TILE], F32, name="result", bufs=4)
@@ -261,9 +264,13 @@ def tile_gptossmlaattention_pb_k_kernel(tc, hidden_states, cos, sin, Wq, bq, gra
         turn(0)
         turn(1)
         multiply_g(0)
+        waiting = []
         for q in range(SLOTS + 4 * TURNED):
             u, phase = divmod(q, TURNED)
             first_even = q % 2 == 0 and phase < 2
+            if phase == 0 and 0 <= u - 3 < UNITS:
+                s, i = divmod(u - 3, PASSES)
+                waiting.extend([(n, i, m) for n in ((2, 1) if s == 1 else (0,)) for m in range(M_TILES)])
             if phase == 0 and u + LOADS_AHEAD < UNITS:
                 load(u + LOADS_AHEAD)
             if phase == 0 and u < UNITS:
@@ -281,12 +288,14 @@ def tile_gptossmlaattention_pb_k_kernel(tc, hidden_states, cos, sin, Wq, bq, gra
                 behind = [b for b in (q - 2, q - 1) if 0 <= b < SLOTS]
                 for b in behind:
                     open_bank(b)
-                if first_even:
-                    if 0 <= u - 3 < UNITS:
-                        s, i = divmod(u - 3, PASSES)
-                        if s == 1:
-                            contract(2, i, plain_codes[i], plain_scales[i])
-                        contract(s, i, rot_codes[u - 3], rot_scales[u - 3])
+                run = 2 if q < SLOTS // SWEEPS else 3
+                for j in range(run):
+                    if waiting:
+                        group, i, m = waiting[0]
+                        waiting.remove((group, i, m))
+                        contract(group, i, m)
+                    elif behind and j < 2 and q < SLOTS // SWEEPS + 8:
+                        keep_warm(dq_ps[behind[0]])
                 for b in behind:
                     add(b)
             if q < SLOTS:

@@ -173,11 +173,12 @@ def tile_gptossmlaattention_pb_k_kernel(tc, hidden_states, cos, sin, Wq, bq, gra
 
         def regroup_g(u):
             by_column(
+                nc.scalar.copy if u < PASSES else nc.vector.tensor_copy,
                 rot_grouped[u][:, TURNED * ROT : N_TILE, :], sums_g[u].rearrange("p (t c) -> p t c", t=PACK)
             )
 
-        def by_column(grouped, rows):
-            nc.scalar.copy(
+        def by_column(copy, grouped, rows):
+            copy(
                 out=grouped.rearrange("p (c i) t -> p c t i", i=4), in_=rows.rearrange("p t (c i) -> p c t i", i=4)
             )
 
@@ -194,7 +195,7 @@ def tile_gptossmlaattention_pb_k_kernel(tc, hidden_states, cos, sin, Wq, bq, gra
 
         def regroup_x(i):
             x_grouped[i] = work.tile([P, HIDDEN, PACK], BF16, name="x_grouped", align_bytes=64)
-            by_column(x_grouped[i][:], x_raw[i][:])
+            by_column(nc.scalar.copy, x_grouped[i][:], x_raw[i][:])
 
         def quantise_x(i):
             x_codes[i] = const.tile([P, HIDDEN], U32, name="x_codes_%d" % i, align_bytes=64)
@@ -260,9 +261,10 @@ def tile_gptossmlaattention_pb_k_kernel(tc, hidden_states, cos, sin, Wq, bq, gra
         negate(0)
         turn_tables(0)
         copy_tables(0)
-        negate(1)
         turn(0)
         turn(1)
+        multiply(0)
+        negate(1)
         multiply_g(0)
         waiting = []
         for q in range(SLOTS + 4 * TURNED):
@@ -288,17 +290,16 @@ def tile_gptossmlaattention_pb_k_kernel(tc, hidden_states, cos, sin, Wq, bq, gra
                 behind = [b for b in (q - 2, q - 1) if 0 <= b < SLOTS]
                 for b in behind:
                     open_bank(b)
-                run = 2 if q < SLOTS // SWEEPS else 3
-                for j in range(run):
-                    if waiting:
-                        group, i, m = waiting[0]
-                        waiting.remove((group, i, m))
-                        contract(group, i, m)
-                    elif behind and j < 2 and q < SLOTS // SWEEPS + 8:
+                if u < 3 and behind:
+                    for j in range(2):
                         keep_warm(dq_ps[behind[0]])
+                run = 2 if q < SLOTS // SWEEPS else 3
+                for group, i, m in waiting[:run]:
+                    contract(group, i, m)
+                waiting = waiting[run:]
                 for b in behind:
                     add(b)
-            if q < SLOTS:
+            if 0 < q < SLOTS:
                 multiply(q)
             if first_even and u + 1 < PASSES:
                 copy_tables(u + 1)
@@ -312,8 +313,10 @@ def tile_gptossmlaattention_pb_k_kernel(tc, hidden_states, cos, sin, Wq, bq, gra
                 if u == PASSES + 2:
                     store(0, 0, nc.scalar.copy)
             if phase == 2:
-                if u < UNITS:
+                if u < PASSES:
                     regroup_g(u)
+                elif PASSES < u <= UNITS:
+                    regroup_g(u - 1)
                 if u + 2 < PASSES:
                     negate(u + 2)
                 if 0 <= u - 2 < UNITS:

@@ -147,7 +147,8 @@ def tile_gptossmlaattention_pb_k_kernel(tc, hidden_states, cos, sin, Wq, bq, gra
 
         def round_off(q):
             u, h = divmod(q, TURNED)
-            nc.scalar.copy(
+            copy = nc.vector.tensor_copy if q == SLOTS - 2 else nc.scalar.copy
+            copy(
                 out=rot_grouped[u][:, h * ROT : (h + 1) * ROT, :], in_=dq_ps[q][:].rearrange("p t j -> p j t")
             )
 
@@ -186,7 +187,8 @@ def tile_gptossmlaattention_pb_k_kernel(tc, hidden_states, cos, sin, Wq, bq, gra
             if half == 0:
                 plain_grouped[i] = work.tile([P, N_TILE, PACK], BF16, name="plain_grouped", align_bytes=64)
             source = plain_raw[i][:] if half == 0 else g[PASSES + i][:, :, :, 0:PLAIN]
-            nc.scalar.copy(
+            copy = nc.vector.tensor_copy if i == PASSES - 1 else nc.scalar.copy
+            copy(
                 out=plain_grouped[i][:, half * UNIT_PLAIN : (half + 1) * UNIT_PLAIN, :].rearrange(
                     "p (h c i) t -> p h c t i", h=UNIT_HEADS, i=4
                 ),
@@ -263,6 +265,8 @@ def tile_gptossmlaattention_pb_k_kernel(tc, hidden_states, cos, sin, Wq, bq, gra
         copy_tables(0)
         turn(0)
         turn(1)
+        for i in range(4):
+            keep_warm(warm)
         multiply(0)
         negate(1)
         multiply_g(0)
@@ -290,7 +294,7 @@ def tile_gptossmlaattention_pb_k_kernel(tc, hidden_states, cos, sin, Wq, bq, gra
                 behind = [b for b in (q - 2, q - 1) if 0 <= b < SLOTS]
                 for b in behind:
                     open_bank(b)
-                if u < 3 and behind:
+                if behind and not waiting and not 3 <= u < PASSES:
                     for j in range(2):
                         keep_warm(dq_ps[behind[0]])
                 run = 2 if q < SLOTS // SWEEPS else 3
@@ -303,12 +307,12 @@ def tile_gptossmlaattention_pb_k_kernel(tc, hidden_states, cos, sin, Wq, bq, gra
                 multiply(q)
             if first_even and u + 1 < PASSES:
                 copy_tables(u + 1)
-            if phase == 0 and PASSES <= u < UNITS:
+            if phase == 0 and PASSES <= u < UNITS - 1:
                 regroup_plain(u - PASSES, 0)
             if phase == 1:
                 if u < PASSES:
                     regroup_x(u)
-                elif u < UNITS:
+                elif u < UNITS - 1:
                     regroup_plain(u - PASSES, 1)
                 if u == PASSES + 2:
                     store(0, 0, nc.scalar.copy)
@@ -319,6 +323,9 @@ def tile_gptossmlaattention_pb_k_kernel(tc, hidden_states, cos, sin, Wq, bq, gra
                     regroup_g(u - 1)
                 if u + 2 < PASSES:
                     negate(u + 2)
+                if u == UNITS - 1:
+                    regroup_plain(PASSES - 1, 0)
+                    regroup_plain(PASSES - 1, 1)
                 if 0 <= u - 2 < UNITS:
                     quantise_rot(u - 2)
                 if 0 <= u - 1 < PASSES:

from contextlib import ExitStack

import concourse.mybir as mybir
from concourse.masks import make_identity

BF16 = mybir.dt.bfloat16
F32 = mybir.dt.float32
U32 = mybir.dt.uint32
U8 = mybir.dt.uint8
E4M3_X4 = mybir.dt.float8_e4m3fn_x4
E5M2_X4 = mybir.dt.float8_e5m2_x4
ALU = mybir.AluOpType

P = 128
PACK = 4
K_PASS = P * PACK

TOKENS = 8192
HIDDEN = 256
HEADS = 8
PLAIN = 64
ROT = 128
HALF = ROT // 2
HEAD_COLS = PLAIN + ROT
DQ_COLS = HEADS * HEAD_COLS

PASSES = TOKENS // K_PASS
SWEEPS = 2
UNIT_HEADS = HEADS // SWEEPS
UNITS = SWEEPS * PASSES
TURNED = 3
SLOTS = UNITS * TURNED
M_TILE = 128
N_TILE = 512
M_TILES = HIDDEN // M_TILE
UNIT_PLAIN = UNIT_HEADS * PLAIN
LOADS_AHEAD = 3

FLOPS = 2 * TOKENS * HIDDEN * DQ_COLS
BYTES = 2 * TOKENS * (HIDDEN + 2 * ROT + DQ_COLS) + 4 * HIDDEN * DQ_COLS


def tile_gptossmlaattention_pb_k_kernel(tc, hidden_states, cos, sin, Wq, bq, grad_out, out):
    nc = tc.nc
    with ExitStack() as stack:
        const = stack.enter_context(tc.tile_pool(name="const", bufs=1))
        loads = stack.enter_context(tc.tile_pool(name="loads", bufs=3))
        work = stack.enter_context(tc.tile_pool(name="work", bufs=3))
        psum = stack.enter_context(tc.psum_pool(name="psum", bufs=1))
        stack.enter_context(tc.manual_schedule())

        ident = const.tile([P, P], BF16, name="ident")
        make_identity(nc, ident[:])
        ident32 = const.tile([P, P], F32, name="ident32")
        make_identity(nc, ident32[:])
        swap32 = const.tile([P, P], F32, name="swap32")
        nc.vector.tensor_copy(out=swap32[:, 0:HALF], in_=ident32[:, HALF:ROT])
        nc.vector.tensor_copy(out=swap32[:, HALF:ROT], in_=ident32[:, 0:HALF])

        tables, turned, tables_ps = {}, {}, {}
        g, x_raw, plain_raw = {}, {}, {}
        r_ps, prods, dq_ps, prods_g, sums_g = {}, {}, {}, {}, {}
        x_grouped, plain_grouped, rot_grouped = {}, {}, {}
        x_codes, x_scales, plain_codes, plain_scales, rot_codes, rot_scales = {}, {}, {}, {}, {}, {}
        acc = {}

        def load(u):
            s, i = divmod(u, PASSES)
            tokens = slice(i * K_PASS, (i + 1) * K_PASS)
            if s == 0:
                tables[i] = const.tile([P, 2, PACK, ROT], BF16, name="tables_%d" % i)
                for w, table in ((1, sin), (0, cos)):
                    nc.sync.dma_start(
                        out=tables[i][:, w, :, :], in_=table[0, tokens, :].rearrange("(p t) j -> p t j", t=PACK)
                    )
            g[u] = loads.tile([P, UNIT_HEADS, PACK, HEAD_COLS], BF16, name="g", bufs=LOADS_AHEAD + 2)
            for h0, h1 in ((0, 1), (1, 4)) if u == 0 else ((0, 4),):
                heads = slice(s * UNIT_HEADS + h0, s * UNIT_HEADS + h1)
                nc.sync.dma_start(
                    out=g[u][:, h0:h1, :, :], in_=grad_out[0, heads, tokens, :].rearrange("h (p t) c -> p h t c", t=PACK)
                )
            if s == 1:
                plain_raw[i] = loads.tile([P, UNIT_HEADS, PACK, PLAIN], BF16, name="plain_raw")
                for h in range(UNIT_HEADS):
                    nc.sync.dma_start(
                        out=plain_raw[i][:, h, :, :],
                        in_=grad_out[0, h, tokens, 0:PLAIN].rearrange("(p t) c -> p t c", t=PACK),
                    )
            if s == 0:
                x_raw[i] = loads.tile([P, PACK, HIDDEN], BF16, name="x_raw")
                nc.sync.dma_start(
                    out=x_raw[i][:], in_=hidden_states[0, tokens, :].rearrange("(p t) c -> p t c", t=PACK)
                )

        def negate(i):
            low = tables[i][:, 1, :, 0:HALF]
            nc.vector.tensor_scalar(out=low, in0=low, scalar1=-1.0, scalar2=0.0, op0=ALU.mult, op1=ALU.add)

        def turn_tables(i):
            tables_ps[i] = psum.tile([P, 2, PACK, P], BF16, name="tables_ps", tag="bank_0")
            for w in (0, 1):
                for t in range(PACK):
                    nc.tensor.transpose(out=tables_ps[i][:, w, t, :], in_=tables[i][:, w, t, :], identity=ident[:])

        def copy_tables(i):
            turned[i] = const.tile([P, 2, PACK, P], BF16, name="turned_%d" % i)
            nc.scalar.copy(out=turned[i][:], in_=tables_ps[i][:])

        def turn(q):
            u, h = divmod(q, TURNED)
            if q % 2 == 0:
                pair = psum.tile([P, 2 * PACK, P], BF16, name="r_ps", bufs=2)
                r_ps[q], r_ps[q + 1] = pair[:, 0:PACK, :], pair[:, PACK:, :]
            for t in range(PACK):
                nc.tensor.transpose(out=r_ps[q][:, t, :], in_=g[u][:, h, t, PLAIN:HEAD_COLS], identity=ident[:])

        def multiply(q):
            i = (q // TURNED) % PASSES
            prods[q] = work.tile([P, 2, PACK, P], F32, name="prods", bufs=6)
            nc.vector.tensor_tensor(
                out=prods[q][:],
                in0=r_ps[q].unsqueeze(1).to_broadcast([P, 2, PACK, P]),
                in1=turned[i][:],
                op=ALU.mult,
            )

        def keep_warm(bank):
            nc.tensor.matmul(
                out=bank[:], lhsT=ident[:], rhs=ident[:].unsqueeze(1).to_broadcast([P, PACK, P]), start=True, stop=True
            )

        def open_bank(q):
            banks = ("dq_0", "dq_1", "bank_1") if q < SLOTS // SWEEPS else ("dq_0", "dq_1")
            dq_ps[q] = psum.tile([P, PACK, ROT], F32, name="dq_ps", tag=banks[q % len(banks)])

        def add(q):
            for t in range(PACK):
                for w, order in ((0, ident32), (1, swap32)):
                    nc.tensor.matmul(
                        out=dq_ps[q][:, t, :],
                        lhsT=prods[q][:, w, t, :],
                        rhs=order[:],
                        start=(w == 0),
                        stop=(w == 1),
                        is_transpose=True,
                    )

        def round_off(q):
            u, h = divmod(q, TURNED)
            copy = nc.vector.tensor_copy if q == SLOTS - 2 else nc.scalar.copy
            copy(
                out=rot_grouped[u][:, h * ROT : (h + 1) * ROT, :], in_=dq_ps[q][:].rearrange("p t j -> p j t")
            )

        def multiply_g(u):
            i = u % PASSES
            prods_g[u] = work.tile([P, 2, PACK, ROT], F32, name="prods_g", bufs=2)
            nc.gpsimd.tensor_tensor(
                out=prods_g[u][:],
                in0=g[u][:, TURNED, :, PLAIN:HEAD_COLS].unsqueeze(1).to_broadcast([P, 2, PACK, ROT]),
                in1=tables[i][:],
                op=ALU.mult,
            )

        def add_g(u):
            rot_grouped[u] = work.tile([P, N_TILE + ROT, PACK], BF16, name="rot_grouped", align_bytes=64)
            sums_g[u] = rot_grouped[u][:, N_TILE:, :].rearrange("p c t -> p (c t)")
            nc.gpsimd.tensor_tensor(
                out=sums_g[u].rearrange("p (t x j) -> p t x j", t=PACK, x=2),
                in0=prods_g[u][:, 0, :, :].rearrange("p t (x j) -> p t x j", x=2),
                in1=prods_g[u][:, 1, :, :].rearrange("p t (x j) -> p t x j", x=2)[:, :, ::-1, :],
                op=ALU.add,
            )

        def regroup_g(u):
            by_column(
                nc.scalar.copy if u < PASSES else nc.vector.tensor_copy,
                rot_grouped[u][:, TURNED * ROT : N_TILE, :], sums_g[u].rearrange("p (t c) -> p t c", t=PACK)
            )

        def by_column(copy, grouped, rows):
            copy(
                out=grouped.rearrange("p (c i) t -> p c t i", i=4), in_=rows.rearrange("p t (c i) -> p c t i", i=4)
            )

        def regroup_plain(i, half):
            if half == 0:
                plain_grouped[i] = work.tile([P, N_TILE, PACK], BF16, name="plain_grouped", align_bytes=64)
            source = plain_raw[i][:] if half == 0 else g[PASSES + i][:, :, :, 0:PLAIN]
            copy = nc.vector.tensor_copy if i == PASSES - 1 else nc.scalar.copy
            copy(
                out=plain_grouped[i][:, half * UNIT_PLAIN : (half + 1) * UNIT_PLAIN, :].rearrange(
                    "p (h c i) t -> p h c t i", h=UNIT_HEADS, i=4
                ),
                in_=source.rearrange("p h t (c i) -> p h c t i", i=4),
            )

        def regroup_x(i):
            x_grouped[i] = work.tile([P, HIDDEN, PACK], BF16, name="x_grouped", align_bytes=64)
            by_column(nc.scalar.copy, x_grouped[i][:], x_raw[i][:])

        def quantise_x(i):
            x_codes[i] = const.tile([P, HIDDEN], U32, name="x_codes_%d" % i, align_bytes=64)
            x_scales[i] = const.tile([P, HIDDEN], U8, name="x_scales_%d" % i, align_bytes=64)
            nc.vector.quantize_mx(
                out=x_codes[i][:].bitcast(E4M3_X4),
                scales=x_scales[i][:],
                in_=x_grouped[i][:].rearrange("p c t -> p (c t)"),
            )

        def quantise_plain(i):
            plain_codes[i] = work.tile([P, N_TILE], U32, name="plain_codes", align_bytes=64)
            plain_scales[i] = work.tile([P, N_TILE], U8, name="plain_scales", align_bytes=64)
            nc.vector.quantize_mx(
                out=plain_codes[i][:].bitcast(E5M2_X4),
                scales=plain_scales[i][:],
                in_=plain_grouped[i][:].rearrange("p c t -> p (c t)"),
            )

        def quantise_rot(u):
            rot_codes[u] = work.tile([P, N_TILE], U32, name="rot_codes", align_bytes=64)
            rot_scales[u] = work.tile([P, N_TILE], U8, name="rot_scales", align_bytes=64)
            nc.vector.quantize_mx(
                out=rot_codes[u][:].bitcast(E5M2_X4),
                scales=rot_scales[u][:],
                in_=rot_grouped[u][:, 0:N_TILE, :].rearrange("p c t -> p (c t)"),
            )

        def contract(group, i, m):
            if group == 2:
                codes, scales = plain_codes[i], plain_scales[i]
            else:
                codes, scales = rot_codes[group * PASSES + i], rot_scales[group * PASSES + i]
            if i == 0:
                bank = m if group == 1 else M_TILES + m
                acc[group, m] = psum.tile([M_TILE, N_TILE], F32, name="acc", tag="bank_%d" % bank)
            m_cols = slice(m * M_TILE, (m + 1) * M_TILE)
            nc.tensor.matmul_mx(
                out=acc[group, m][:],
                lhsT=x_codes[i][:, m_cols].bitcast(E4M3_X4),
                lhsT_scale=x_scales[i][:, m_cols],
                rhs=codes[:].bitcast(E5M2_X4),
                rhs_scale=scales[:],
                start=(i == 0),
                stop=(i == PASSES - 1),
            )

        def store(group, m, copy):
            result = work.tile([M_TILE, N_TILE], F32, name="result", bufs=4)
            copy(out=result[:], in_=acc[group, m][:])
            by_head = out[m * M_TILE : (m + 1) * M_TILE, :].rearrange("m (h c) -> m h c", h=HEADS)
            if group == 2:
                to, heads = by_head[:, :, 0:PLAIN], HEADS
            else:
                to, heads = by_head[:, group * UNIT_HEADS : (group + 1) * UNIT_HEADS, PLAIN:HEAD_COLS], UNIT_HEADS
            nc.sync.dma_start(out=to, in_=result[:].rearrange("m (h c) -> m h c", h=heads))

        for u in range(LOADS_AHEAD):
            load(u)
        warm = psum.tile([P, PACK, ROT], F32, name="warm", tag="dq_0")
        for i in range(6):
            keep_warm(warm)
        negate(0)
        turn_tables(0)
        copy_tables(0)
        turn(0)
        turn(1)
        for i in range(4):
            keep_warm(warm)
        multiply(0)
        negate(1)
        multiply_g(0)
        waiting = []
        for q in range(SLOTS + 4 * TURNED):
            u, phase = divmod(q, TURNED)
            first_even = q % 2 == 0 and phase < 2
            if phase == 0 and 0 <= u - 3 < UNITS:
                s, i = divmod(u - 3, PASSES)
                waiting.extend([(n, i, m) for n in ((2, 1) if s == 1 else (0,)) for m in range(M_TILES)])
            if phase == 0 and u + LOADS_AHEAD < UNITS:
                load(u + LOADS_AHEAD)
            if phase == 0 and u < UNITS:
                add_g(u)
                if u + 1 < UNITS:
                    multiply_g(u + 1)
            if 0 <= q - 3 < SLOTS:
                round_off(q - 3)
            if q % 2 == 0:
                for ahead in (q + 2, q + 3):
                    if ahead < SLOTS:
                        turn(ahead)
                if first_even and u + 1 < PASSES:
                    turn_tables(u + 1)
                behind = [b for b in (q - 2, q - 1) if 0 <= b < SLOTS]
                for b in behind:
                    open_bank(b)
                if behind and not waiting and not 3 <= u < PASSES:
                    for j in range(2):
                        keep_warm(dq_ps[behind[0]])
                run = 2 if q < SLOTS // SWEEPS else 3
                for group, i, m in waiting[:run]:
                    contract(group, i, m)
                waiting = waiting[run:]
                for b in behind:
                    add(b)
            if 0 < q < SLOTS:
                multiply(q)
            if first_even and u + 1 < PASSES:
                copy_tables(u + 1)
            if phase == 0 and PASSES <= u < UNITS - 1:
                regroup_plain(u - PASSES, 0)
            if phase == 1:
                if u < PASSES:
                    regroup_x(u)
                elif u < UNITS - 1:
                    regroup_plain(u - PASSES, 1)
                if u == PASSES + 2:
                    store(0, 0, nc.scalar.copy)
            if phase == 2:
                if u < PASSES:
                    regroup_g(u)
                elif PASSES < u <= UNITS:
                    regroup_g(u - 1)
                if u + 2 < PASSES:
                    negate(u + 2)
                if u == UNITS - 1:
                    regroup_plain(PASSES - 1, 0)
                    regroup_plain(PASSES - 1, 1)
                if 0 <= u - 2 < UNITS:
                    quantise_rot(u - 2)
                if 0 <= u - 1 < PASSES:
                    quantise_x(u - 1)
                if PASSES <= u - 1 < UNITS:
                    quantise_plain(u - 1 - PASSES)
                if u == PASSES + 2:
                    store(0, 1, nc.scalar.copy)

        for group in (2, 1):
            store(group, 0, nc.vector.tensor_copy)
            store(group, 1, nc.scalar.copy)
